import numpy as np
import ml_dtypes


def mxq(x, axis, fmt="e4m3"):
    dtype, down = {"e4m3": (ml_dtypes.float8_e4m3fn, 7), "e5m2": (ml_dtypes.float8_e5m2, 14)}[fmt]
    v = np.moveaxis(np.asarray(x, np.float32).astype(ml_dtypes.bfloat16).astype(np.float64), axis, -1)
    blocks = v.reshape(v.shape[:-1] + (-1, 32))
    amax = np.abs(blocks).max(-1, keepdims=True)
    byte = np.maximum(np.where(amax > 0, np.frexp(amax)[1] - 1 + 127, 0) - down, 1)
    scale = np.exp2(byte - 127.0)
    codes = (blocks / scale).astype(np.float32).astype(dtype).astype(np.float64)
    return np.moveaxis((codes * scale).reshape(v.shape), -1, axis)


WIDE = False


def mx_kscale(k):
    if not WIDE:
        return np.ones(k)
    levels = np.array([10, -10, 5, -5, 0])
    if k % 512:
        return np.exp2(np.random.permutation(np.resize(levels, k // 32))).repeat(32)
    a = np.empty((k // 512, 16))
    for p in range(k // 512):
        a[p, :8] = np.random.permutation(np.resize(levels, 8))
        for g in range(8):
            far = levels[np.abs(levels - a[p, g]) >= 10]
            a[p, g + 8] = far[np.random.randint(len(far))]
    return np.exp2(a.ravel()).repeat(32)


BF16 = ml_dtypes.bfloat16


def bf(x):
    return np.asarray(x, np.float32).astype(BF16)


def f64(x):
    return np.asarray(x).astype(np.float64)


B, T, E, V, NH, C = 1, 1024, 1024, 2048, 4, 512
KD = E // NH
SCALING = KD ** -0.5


def rotate_every_two(x):
    x1 = x[..., 0::2]
    x2 = x[..., 1::2]
    return np.stack((-x2, x1), axis=-1).reshape(x.shape)


def theta_shift(x, sin, cos):
    return x * cos + rotate_every_two(x) * sin


def rope_tables():
    half = np.arange(0, KD, 2) / KD
    angle = np.repeat(1.0 / 10000.0 ** half, 2)
    pos = np.arange(T)
    return np.sin(pos[:, None] * angle[None, :]), np.cos(pos[:, None] * angle[None, :])


def setup_inputs():
    s = mx_kscale(E)
    sin, cos = rope_tables()
    return {"hidden_states": bf(np.random.standard_normal((B, T, E)) * s),
            "wq": bf(np.random.standard_normal((E, E)) / np.sqrt(E) / s[None, :]),
            "wk": bf(np.random.standard_normal((E, E)) * 2.0 / np.sqrt(E) / s[None, :]),
            "sin": bf(sin), "cos": bf(cos)}


def reference(hidden_states, wq, wk, sin, cos):
    xq = mxq(f64(hidden_states), 2, "e4m3")
    q = xq @ mxq(f64(wq), 1, "e4m3").T
    k = xq @ mxq(f64(wk), 1, "e4m3").T
    q = q.reshape(B, T, NH, KD).transpose(0, 2, 1, 3)
    k = k.reshape(B, T, NH, KD).transpose(0, 2, 1, 3) * SCALING
    return theta_shift(q, f64(sin), f64(cos)), theta_shift(k, f64(sin), f64(cos))

@@ -1,0 +1,220 @@
+from contextlib import ExitStack
+
+import concourse.mybir as mybir
+from concourse.masks import make_identity
+
+F32 = mybir.dt.float32
+BF16 = mybir.dt.bfloat16
+U32 = mybir.dt.uint32
+U8 = mybir.dt.uint8
+FP8X4 = mybir.dt.float8_e4m3fn_x4
+MULT = mybir.AluOpType.mult
+ADD = mybir.AluOpType.add
+
+P = 128
+TOKENS = 1024
+K = 1024
+HEADS = 4
+HEAD_DIM = 256
+BLOCK = 512
+BLOCK_HEADS = BLOCK // HEAD_DIM
+BLOCKS = HEADS * HEAD_DIM // BLOCK
+ROW_TILES = BLOCK // P
+K_PASS = 4 * P
+PASSES = K // K_PASS
+HALVES = 2
+TOKEN_TILES = TOKENS // P
+COUPLE = 2
+COUPLES = TOKEN_TILES // COUPLE
+TABLE_PARTS = 2
+PART_TILES = TOKEN_TILES // TABLE_PARTS
+K_SCALING = HEAD_DIM ** -0.5
+GPSIMD_COUPLES = 13
+
+FLOPS = 2 * TOKENS * K * (2 * HEADS * HEAD_DIM)
+
+
+def k_onto_partitions(nc, banks, identity, rows, grouped_words):
+    words = rows.bitcast(F32)
+    turned = banks.tile([P, PASSES, HALVES, P], F32)
+    for g in range(PASSES):
+        for u in range(HALVES):
+            every_second = words[:, g * HALVES * P + u : (g + 1) * HALVES * P : HALVES]
+            nc.tensor.transpose(turned[:, g, u, :], every_second, identity)
+    nc.scalar.copy(out=grouped_words, in_=turned[:].rearrange("p g u r -> p g r u"))
+
+
+def pairs(columns):
+    return columns.rearrange("p h (i e) -> p h i e", e=2)
+
+
+def for_each_head(table, n):
+    one_head = table[:, n, :].rearrange("p (i e) -> p i e", e=2)
+    return one_head.unsqueeze(1).to_broadcast([P, BLOCK_HEADS, HEAD_DIM // 2, 2])
+
+
+def tile_nucleusxmultiscaleretention_pa_kernel(
+    tc, hidden_states, wq, wk, sin, cos, out_0, out_1
+):
+    nc = tc.nc
+    weights = [wq, wk]
+    scalings = [1.0, K_SCALING]
+
+    token_rows = hidden_states[0].rearrange("(p n) k -> n p k", n=TOKEN_TILES)
+    weight_rows = [w.rearrange("(c j r) k -> c j r k", c=BLOCKS, j=ROW_TILES) for w in weights]
+    cos_rows = cos.rearrange("(p n) d -> p n d", n=TOKEN_TILES)
+    sin_rows = sin.rearrange("(p n) d -> p n d", n=TOKEN_TILES)
+    out_rows = [
+        o[0].rearrange("(c h) (p a t) d -> c a p h (t d)", c=BLOCKS, a=COUPLES, t=COUPLE)
+        for o in (out_0, out_1)
+    ]
+
+    with ExitStack() as ctx:
+        keep = ctx.enter_context(tc.tile_pool(name="keep", bufs=1))
+        stage_tokens = ctx.enter_context(tc.tile_pool(name="stage_tokens", bufs=3))
+        stage_block = ctx.enter_context(tc.tile_pool(name="stage_block", bufs=2))
+        products = ctx.enter_context(tc.tile_pool(name="products", bufs=4))
+        results = ctx.enter_context(tc.tile_pool(name="results", bufs=4))
+        turn_banks = ctx.enter_context(tc.psum_pool(name="turn_banks", bufs=4))
+        block_banks = ctx.enter_context(tc.psum_pool(name="block_banks", bufs=4))
+
+        identity = keep.tile([P, P], F32)
+        make_identity(nc, identity[:])
+
+        raw_tokens = [
+            keep.tile([P, K], BF16, name="raw_tokens%d" % n) for n in range(TOKEN_TILES)
+        ]
+        raw_block = [
+            [
+                [keep.tile([P, K], BF16, name="raw_w%d_%d_%d" % (m, c, j)) for j in range(ROW_TILES)]
+                for c in range(BLOCKS)
+            ]
+            for m in range(2)
+        ]
+        cos_sb = keep.tile([P, TOKEN_TILES, HEAD_DIM], BF16)
+        sin_sb = keep.tile([P, TOKEN_TILES, HEAD_DIM], BF16)
+
+        token_codes = keep.tile([P, TOKEN_TILES, PASSES * P], U32, align_bytes=64)
+        token_scales = keep.tile([P, TOKEN_TILES, PASSES * P], U8, align_bytes=64)
+        block_codes = [
+            [
+                keep.tile([P, PASSES, BLOCK], U32, name="codes%d_%d" % (m, c), align_bytes=64)
+                for c in range(BLOCKS)
+            ]
+            for m in range(2)
+        ]
+        block_scales = [
+            [
+                keep.tile([P, PASSES, BLOCK], U8, name="scales%d_%d" % (m, c), align_bytes=64)
+                for c in range(BLOCKS)
+            ]
+            for m in range(2)
+        ]
+
+        def load_tokens(n):
+            nc.sync.dma_start(out=raw_tokens[n][:], in_=token_rows[n])
+
+        def load_block(m, c):
+            for j in range(ROW_TILES):
+                nc.sync.dma_start(out=raw_block[m][c][j][:], in_=weight_rows[m][c, j])
+
+        def load_tables(part):
+            tiles = slice(part * PART_TILES, (part + 1) * PART_TILES)
+            nc.sync.dma_start(out=cos_sb[:, tiles, :], in_=cos_rows[:, tiles, :])
+            nc.sync.dma_start(out=sin_sb[:, tiles, :], in_=sin_rows[:, tiles, :])
+            even = sin_sb[:, tiles, :].rearrange("p n (i e) -> p (n i) e", e=2)[:, :, 0]
+            nc.gpsimd.tensor_scalar(
+                out=even, in0=even, scalar1=-1.0, scalar2=0.0, op0=MULT, op1=ADD
+            )
+
+        load_block(0, 0)
+        for part in range(TABLE_PARTS):
+            load_tables(part)
+            for n in range(part * PART_TILES, (part + 1) * PART_TILES):
+                load_tokens(n)
+        load_block(0, 1)
+        load_block(1, 0)
+        load_block(1, 1)
+
+        def quantise_tokens(n):
+            grouped = stage_tokens.tile([P, PASSES * P * 4], BF16, align_bytes=64)
+            k_onto_partitions(
+                nc,
+                turn_banks,
+                identity[:],
+                raw_tokens[n][:],
+                grouped[:].bitcast(F32).rearrange("p (g r u) -> p g r u", g=PASSES, u=HALVES),
+            )
+            nc.vector.quantize_mx(
+                out=token_codes[:, n, :].bitcast(FP8X4),
+                scales=token_scales[:, n, :],
+                in_=grouped[:],
+            )
+
+        def quantise_block(m, c):
+            grouped = stage_block.tile([P, PASSES * BLOCK * 4], BF16, align_bytes=64)
+            grouped_words = grouped[:].bitcast(F32).rearrange(
+                "p (g j r u) -> p g j r u", g=PASSES, j=ROW_TILES, u=HALVES
+            )
+            for j in range(ROW_TILES):
+                k_onto_partitions(
+                    nc, turn_banks, identity[:], raw_block[m][c][j][:], grouped_words[:, :, j, :, :]
+                )
+            width = BLOCK * 4
+            for g in range(PASSES):
+                nc.vector.quantize_mx(
+                    out=block_codes[m][c][:, g, :].bitcast(FP8X4),
+                    scales=block_scales[m][c][:, g, :],
+                    in_=grouped[:, g * width : (g + 1) * width],
+                )
+
+        def multiply(m, c, n, with_cos, with_sin):
+            bank = block_banks.tile([P, BLOCK_HEADS, HEAD_DIM], F32)
+            for g in range(PASSES):
+                tokens = slice(g * P, (g + 1) * P)
+                nc.tensor.matmul_mx(
+                    out=bank[:].rearrange("p h d -> p (h d)"),
+                    lhsT=token_codes[:, n, tokens].bitcast(FP8X4),
+                    lhsT_scale=token_scales[:, n, tokens],
+                    rhs=block_codes[m][c][:, g, :].bitcast(FP8X4),
+                    rhs_scale=block_scales[m][c][:, g, :],
+                    start=(g == 0),
+                    stop=(g == PASSES - 1),
+                )
+            nc.vector.scalar_tensor_tensor(
+                out=pairs(with_cos),
+                in0=pairs(bank[:]),
+                scalar=scalings[m],
+                in1=for_each_head(cos_sb, n),
+                op0=MULT,
+                op1=MULT,
+            )
+            nc.vector.scalar_tensor_tensor(
+                out=pairs(with_sin),
+                in0=pairs(bank[:])[:, :, :, ::-1],
+                scalar=scalings[m],
+                in1=for_each_head(sin_sb, n),
+                op0=MULT,
+                op1=MULT,
+            )
+
+        blocks = [(m, c) for m in range(2) for c in range(BLOCKS)]
+        quantise_block(0, 0)
+        quantise_tokens(0)
+        for index, (m, c) in enumerate(blocks):
+            for a in range(COUPLES):
+                with_cos = products.tile([P, BLOCK_HEADS, COUPLE, HEAD_DIM], F32)
+                with_sin = products.tile([P, BLOCK_HEADS, COUPLE, HEAD_DIM], F32)
+                for t in range(COUPLE):
+                    n = a * COUPLE + t
+                    if index == 0 and n + 1 < TOKEN_TILES:
+                        quantise_tokens(n + 1)
+                    multiply(m, c, n, with_cos[:, :, t, :], with_sin[:, :, t, :])
+                rotated = results.tile([P, BLOCK_HEADS, COUPLE, HEAD_DIM], F32)
+                adder = nc.gpsimd if index * COUPLES + a < GPSIMD_COUPLES else nc.vector
+                adder.tensor_tensor(out=rotated[:], in0=with_cos[:], in1=with_sin[:], op=ADD)
+                nc.sync.dma_start(
+                    out=out_rows[m][c, a], in_=rotated[:].rearrange("p h t d -> p h (t d)")
+                )
+                if a == 0 and index + 1 < len(blocks):
+                    quantise_block(blocks[index + 1][0], blocks[index + 1][1])

@@ -20,48 +20,29 @@ BLOCK = 512
 BLOCK_HEADS = BLOCK // HEAD_DIM
 BLOCKS = HEADS * HEAD_DIM // BLOCK
 ROW_TILES = BLOCK // P
+HEAD_ROW_TILES = HEAD_DIM // P
 K_PASS = 4 * P
 PASSES = K // K_PASS
 HALVES = 2
 TOKEN_TILES = TOKENS // P
 COUPLE = 2
 COUPLES = TOKEN_TILES // COUPLE
-TABLE_PARTS = 2
-PART_TILES = TOKEN_TILES // TABLE_PARTS
 K_SCALING = HEAD_DIM ** -0.5
-GPSIMD_COUPLES = 13
 
 FLOPS = 2 * TOKENS * K * (2 * HEADS * HEAD_DIM)
-
-
-def k_onto_partitions(nc, banks, identity, rows, grouped_words):
-    words = rows.bitcast(F32)
-    turned = banks.tile([P, PASSES, HALVES, P], F32)
-    for g in range(PASSES):
-        for u in range(HALVES):
-            every_second = words[:, g * HALVES * P + u : (g + 1) * HALVES * P : HALVES]
-            nc.tensor.transpose(turned[:, g, u, :], every_second, identity)
-    nc.scalar.copy(out=grouped_words, in_=turned[:].rearrange("p g u r -> p g r u"))
-
-
-def pairs(columns):
-    return columns.rearrange("p h (i e) -> p h i e", e=2)
-
-
-def for_each_head(table, n):
-    one_head = table[:, n, :].rearrange("p (i e) -> p i e", e=2)
-    return one_head.unsqueeze(1).to_broadcast([P, BLOCK_HEADS, HEAD_DIM // 2, 2])
 
 
 def tile_nucleusxmultiscaleretention_pa_kernel(
     tc, hidden_states, wq, wk, sin, cos, out_0, out_1
 ):
     nc = tc.nc
-    weights = [wq, wk]
     scalings = [1.0, K_SCALING]
+    blocks = [(m, c) for m in range(2) for c in range(BLOCKS)]
 
-    token_rows = hidden_states[0].rearrange("(p n) k -> n p k", n=TOKEN_TILES)
-    weight_rows = [w.rearrange("(c j r) k -> c j r k", c=BLOCKS, j=ROW_TILES) for w in weights]
+    token_rows = hidden_states[0].rearrange("(p n) k -> p n k", n=TOKEN_TILES)
+    weight_rows = [
+        w.rearrange("(c j r) k -> c r j k", c=BLOCKS, j=ROW_TILES) for w in (wq, wk)
+    ]
     cos_rows = cos.rearrange("(p n) d -> p n d", n=TOKEN_TILES)
     sin_rows = sin.rearrange("(p n) d -> p n d", n=TOKEN_TILES)
     out_rows = [
@@ -74,147 +55,296 @@ def tile_nucleusxmultiscaleretention_pa_kernel(
         stage_tokens = ctx.enter_context(tc.tile_pool(name="stage_tokens", bufs=3))
         stage_block = ctx.enter_context(tc.tile_pool(name="stage_block", bufs=2))
         products = ctx.enter_context(tc.tile_pool(name="products", bufs=4))
-        results = ctx.enter_context(tc.tile_pool(name="results", bufs=4))
+        results = ctx.enter_context(tc.tile_pool(name="results", bufs=6))
         turn_banks = ctx.enter_context(tc.psum_pool(name="turn_banks", bufs=4))
         block_banks = ctx.enter_context(tc.psum_pool(name="block_banks", bufs=4))
+        ctx.enter_context(tc.manual_schedule())
 
         identity = keep.tile([P, P], F32)
         make_identity(nc, identity[:])
 
         raw_tokens = [
-            keep.tile([P, K], BF16, name="raw_tokens%d" % n) for n in range(TOKEN_TILES)
+            keep.tile([P, COUPLE, K], BF16, name="raw_tokens%d" % a) for a in range(COUPLES)
         ]
         raw_block = [
             [
-                [keep.tile([P, K], BF16, name="raw_w%d_%d_%d" % (m, c, j)) for j in range(ROW_TILES)]
-                for c in range(BLOCKS)
+                keep.tile([P, HEAD_ROW_TILES, K], BF16, name="raw_w%d_%d" % (b, h))
+                for h in range(BLOCK_HEADS)
             ]
-            for m in range(2)
+            for b in range(len(blocks))
         ]
         cos_sb = keep.tile([P, TOKEN_TILES, HEAD_DIM], BF16)
         sin_sb = keep.tile([P, TOKEN_TILES, HEAD_DIM], BF16)
 
-        token_codes = keep.tile([P, TOKEN_TILES, PASSES * P], U32, align_bytes=64)
-        token_scales = keep.tile([P, TOKEN_TILES, PASSES * P], U8, align_bytes=64)
+        token_codes = [
+            keep.tile([P, COUPLE, PASSES * P], U32, name="token_codes%d" % a, align_bytes=64)
+            for a in range(COUPLES)
+        ]
+        token_scales = [
+            keep.tile([P, COUPLE, PASSES * P], U8, name="token_scales%d" % a, align_bytes=64)
+            for a in range(COUPLES)
+        ]
         block_codes = [
-            [
-                keep.tile([P, PASSES, BLOCK], U32, name="codes%d_%d" % (m, c), align_bytes=64)
-                for c in range(BLOCKS)
-            ]
-            for m in range(2)
+            keep.tile([P, PASSES, BLOCK], U32, name="block_codes%d" % b, align_bytes=64)
+            for b in range(len(blocks))
         ]
         block_scales = [
-            [
-                keep.tile([P, PASSES, BLOCK], U8, name="scales%d_%d" % (m, c), align_bytes=64)
-                for c in range(BLOCKS)
-            ]
-            for m in range(2)
+            keep.tile([P, PASSES, BLOCK], U8, name="block_scales%d" % b, align_bytes=64)
+            for b in range(len(blocks))
         ]
 
-        def load_tokens(n):
-            nc.sync.dma_start(out=raw_tokens[n][:], in_=token_rows[n])
+        def load_tokens(a, t0, t1):
+            nc.sync.dma_start(
+                out=raw_tokens[a][:, t0:t1, :],
+                in_=token_rows[:, a * COUPLE + t0 : a * COUPLE + t1, :],
+            )
 
-        def load_block(m, c):
-            for j in range(ROW_TILES):
-                nc.sync.dma_start(out=raw_block[m][c][j][:], in_=weight_rows[m][c, j])
+        def load_rows(b, h, j0, j1):
+            m, c = blocks[b]
+            first = h * HEAD_ROW_TILES
+            nc.sync.dma_start(
+                out=raw_block[b][h][:, j0:j1, :],
+                in_=weight_rows[m][c, :, first + j0 : first + j1, :],
+            )
 
-        def load_tables(part):
-            tiles = slice(part * PART_TILES, (part + 1) * PART_TILES)
-            nc.sync.dma_start(out=cos_sb[:, tiles, :], in_=cos_rows[:, tiles, :])
-            nc.sync.dma_start(out=sin_sb[:, tiles, :], in_=sin_rows[:, tiles, :])
-            even = sin_sb[:, tiles, :].rearrange("p n (i e) -> p (n i) e", e=2)[:, :, 0]
+        def load_tables(n0, n1):
+            nc.sync.dma_start(out=cos_sb[:, n0:n1, :], in_=cos_rows[:, n0:n1, :])
+            nc.sync.dma_start(out=sin_sb[:, n0:n1, :], in_=sin_rows[:, n0:n1, :])
+
+        def negate_even_sines(n0, n1):
+            even = sin_sb[:, n0:n1, :].rearrange("p n (i e) -> p (n i) e", e=2)[:, :, 0]
             nc.gpsimd.tensor_scalar(
                 out=even, in0=even, scalar1=-1.0, scalar2=0.0, op0=MULT, op1=ADD
             )
 
-        load_block(0, 0)
-        for part in range(TABLE_PARTS):
-            load_tables(part)
-            for n in range(part * PART_TILES, (part + 1) * PART_TILES):
-                load_tokens(n)
-        load_block(0, 1)
-        load_block(1, 0)
-        load_block(1, 1)
+        def turn(rows, grouped_words, copy):
+            words = rows.bitcast(F32)
+            turned = turn_banks.tile([P, PASSES, HALVES, P], F32)
+            for g in range(PASSES):
+                for u in range(HALVES):
+                    every_second = words[:, g * HALVES * P + u : (g + 1) * HALVES * P : HALVES]
+                    nc.tensor.transpose(turned[:, g, u, :], every_second, identity[:])
+            copy(out=grouped_words, in_=turned[:].rearrange("p g u r -> p g r u"))
 
-        def quantise_tokens(n):
-            grouped = stage_tokens.tile([P, PASSES * P * 4], BF16, align_bytes=64)
-            k_onto_partitions(
-                nc,
-                turn_banks,
-                identity[:],
-                raw_tokens[n][:],
-                grouped[:].bitcast(F32).rearrange("p (g r u) -> p g r u", g=PASSES, u=HALVES),
+        grouped_tokens = {}
+        grouped_block = {}
+
+        def turn_token(n, copy):
+            a, t = divmod(n, COUPLE)
+            if t == 0:
+                grouped_couple = stage_tokens.tile([P, COUPLE, PASSES * P * 4], BF16, align_bytes=64)
+                grouped_tokens[a] = grouped_couple
+            view = grouped_tokens[a][:, t, :].bitcast(F32)
+            turn(
+                raw_tokens[a][:, t, :],
+                view.rearrange("p (g r u) -> p g r u", g=PASSES, u=HALVES),
+                copy,
             )
+
+        def quantise_tokens(a, t0, t1):
             nc.vector.quantize_mx(
-                out=token_codes[:, n, :].bitcast(FP8X4),
-                scales=token_scales[:, n, :],
-                in_=grouped[:],
+                out=token_codes[a][:, t0:t1, :].rearrange("p t w -> p (t w)").bitcast(FP8X4),
+                scales=token_scales[a][:, t0:t1, :].rearrange("p t w -> p (t w)"),
+                in_=grouped_tokens[a][:, t0:t1, :].rearrange("p t w -> p (t w)"),
             )
 
-        def quantise_block(m, c):
-            grouped = stage_block.tile([P, PASSES * BLOCK * 4], BF16, align_bytes=64)
-            grouped_words = grouped[:].bitcast(F32).rearrange(
+        def turn_rows(b, j, copy):
+            if j == 0:
+                grouped = stage_block.tile([P, PASSES * BLOCK * 4], BF16, align_bytes=64)
+                grouped_block[b] = grouped
+            words = grouped_block[b][:].bitcast(F32).rearrange(
                 "p (g j r u) -> p g j r u", g=PASSES, j=ROW_TILES, u=HALVES
             )
-            for j in range(ROW_TILES):
-                k_onto_partitions(
-                    nc, turn_banks, identity[:], raw_block[m][c][j][:], grouped_words[:, :, j, :, :]
-                )
-            width = BLOCK * 4
+            h, i = divmod(j, HEAD_ROW_TILES)
+            turn(raw_block[b][h][:, i, :], words[:, :, j, :, :], copy)
+
+        def quantise_block(b):
+            nc.vector.quantize_mx(
+                out=block_codes[b][:].rearrange("p g f -> p (g f)").bitcast(FP8X4),
+                scales=block_scales[b][:].rearrange("p g f -> p (g f)"),
+                in_=grouped_block[b][:],
+            )
+
+        def quantise_head(b, h):
+            columns = slice(h * HEAD_DIM, (h + 1) * HEAD_DIM)
             for g in range(PASSES):
+                first = (g * BLOCK + h * HEAD_DIM) * 4
                 nc.vector.quantize_mx(
-                    out=block_codes[m][c][:, g, :].bitcast(FP8X4),
-                    scales=block_scales[m][c][:, g, :],
-                    in_=grouped[:, g * width : (g + 1) * width],
+                    out=block_codes[b][:, g, columns].bitcast(FP8X4),
+                    scales=block_scales[b][:, g, columns],
+                    in_=grouped_block[b][:, first : first + HEAD_DIM * 4],
                 )
 
-        def multiply(m, c, n, with_cos, with_sin):
-            bank = block_banks.tile([P, BLOCK_HEADS, HEAD_DIM], F32)
+        def product(out, b, n, f0, f1):
+            a, t = divmod(n, COUPLE)
             for g in range(PASSES):
                 tokens = slice(g * P, (g + 1) * P)
                 nc.tensor.matmul_mx(
-                    out=bank[:].rearrange("p h d -> p (h d)"),
-                    lhsT=token_codes[:, n, tokens].bitcast(FP8X4),
-                    lhsT_scale=token_scales[:, n, tokens],
-                    rhs=block_codes[m][c][:, g, :].bitcast(FP8X4),
-                    rhs_scale=block_scales[m][c][:, g, :],
+                    out=out,
+                    lhsT=token_codes[a][:, t, tokens].bitcast(FP8X4),
+                    lhsT_scale=token_scales[a][:, t, tokens],
+                    rhs=block_codes[b][:, g, f0:f1].bitcast(FP8X4),
+                    rhs_scale=block_scales[b][:, g, f0:f1],
                     start=(g == 0),
                     stop=(g == PASSES - 1),
                 )
+
+        def pairs(view):
+            return view.rearrange("p x (i e) -> p x i e", e=2)
+
+        def rotate(m, bank, cos_view, sin_view, with_cos, with_sin):
             nc.vector.scalar_tensor_tensor(
-                out=pairs(with_cos),
-                in0=pairs(bank[:]),
-                scalar=scalings[m],
-                in1=for_each_head(cos_sb, n),
-                op0=MULT,
-                op1=MULT,
+                out=pairs(with_cos), in0=pairs(bank), scalar=scalings[m], in1=cos_view,
+                op0=MULT, op1=MULT,
             )
             nc.vector.scalar_tensor_tensor(
-                out=pairs(with_sin),
-                in0=pairs(bank[:])[:, :, :, ::-1],
-                scalar=scalings[m],
-                in1=for_each_head(sin_sb, n),
-                op0=MULT,
-                op1=MULT,
+                out=pairs(with_sin), in0=pairs(bank)[:, :, :, ::-1], scalar=scalings[m],
+                in1=sin_view, op0=MULT, op1=MULT,
             )
 
-        blocks = [(m, c) for m in range(2) for c in range(BLOCKS)]
-        quantise_block(0, 0)
-        quantise_tokens(0)
-        for index, (m, c) in enumerate(blocks):
-            for a in range(COUPLES):
-                with_cos = products.tile([P, BLOCK_HEADS, COUPLE, HEAD_DIM], F32)
-                with_sin = products.tile([P, BLOCK_HEADS, COUPLE, HEAD_DIM], F32)
-                for t in range(COUPLE):
-                    n = a * COUPLE + t
-                    if index == 0 and n + 1 < TOKEN_TILES:
-                        quantise_tokens(n + 1)
-                    multiply(m, c, n, with_cos[:, :, t, :], with_sin[:, :, t, :])
-                rotated = results.tile([P, BLOCK_HEADS, COUPLE, HEAD_DIM], F32)
-                adder = nc.gpsimd if index * COUPLES + a < GPSIMD_COUPLES else nc.vector
-                adder.tensor_tensor(out=rotated[:], in0=with_cos[:], in1=with_sin[:], op=ADD)
-                nc.sync.dma_start(
-                    out=out_rows[m][c, a], in_=rotated[:].rearrange("p h t d -> p h (t d)")
-                )
-                if a == 0 and index + 1 < len(blocks):
-                    quantise_block(blocks[index + 1][0], blocks[index + 1][1])
+        def table_for_heads(table, n):
+            one_head = table[:, n, :].rearrange("p (i e) -> p i e", e=2)
+            return one_head.unsqueeze(1).to_broadcast([P, BLOCK_HEADS, HEAD_DIM // 2, 2])
+
+        state = {}
+
+        def multiply_couple(s):
+            b, a = divmod(s, COUPLES)
+            banks = []
+            for t in range(COUPLE):
+                bank = block_banks.tile([P, BLOCK_HEADS, HEAD_DIM], F32)
+                product(bank[:].rearrange("p h d -> p (h d)"), b, a * COUPLE + t, 0, BLOCK)
+                banks.append(bank)
+            state[s] = banks
+
+        def multiply_heads(s, h):
+            b, a = divmod(s, COUPLES)
+            bank = block_banks.tile([P, BLOCK_HEADS, HEAD_DIM], F32)
+            for t in range(COUPLE):
+                product(bank[:, t, :], b, a * COUPLE + t, h * HEAD_DIM, (h + 1) * HEAD_DIM)
+            state[s, h] = bank
+
+        def new_products(s):
+            with_cos = products.tile([P, BLOCK_HEADS, COUPLE, HEAD_DIM], F32)
+            with_sin = products.tile([P, BLOCK_HEADS, COUPLE, HEAD_DIM], F32)
+            rotated = results.tile([P, BLOCK_HEADS, COUPLE, HEAD_DIM], F32)
+            state["products", s] = (with_cos, with_sin, rotated)
+
+        def rotate_tile(s, t):
+            b, a = divmod(s, COUPLES)
+            n = a * COUPLE + t
+            with_cos, with_sin, rotated = state["products", s]
+            rotate(
+                blocks[b][0], state[s][t][:], table_for_heads(cos_sb, n), table_for_heads(sin_sb, n),
+                with_cos[:, :, t, :], with_sin[:, :, t, :],
+            )
+
+        def rotate_head(s, h):
+            b, a = divmod(s, COUPLES)
+            tiles = slice(a * COUPLE, (a + 1) * COUPLE)
+            with_cos, with_sin, rotated = state["products", s]
+            rotate(
+                blocks[b][0], state[s, h][:], pairs(cos_sb[:, tiles, :]), pairs(sin_sb[:, tiles, :]),
+                with_cos[:, h, :, :], with_sin[:, h, :, :],
+            )
+
+        def add(s, engine, h0, h1):
+            with_cos, with_sin, rotated = state["products", s]
+            engine.tensor_tensor(
+                out=rotated[:, h0:h1, :, :], in0=with_cos[:, h0:h1, :, :],
+                in1=with_sin[:, h0:h1, :, :], op=ADD,
+            )
+
+        def store(s, h0, h1):
+            b, a = divmod(s, COUPLES)
+            m, c = blocks[b]
+            rotated = state["products", s][2]
+            nc.sync.dma_start(
+                out=out_rows[m][c, a][:, h0:h1, :],
+                in_=rotated[:, h0:h1, :, :].rearrange("p h t d -> p h (t d)"),
+            )
+
+        by_scalar = nc.scalar.copy
+        by_vector = nc.vector.tensor_copy
+
+        load_rows(0, 0, 0, 1)
+        load_rows(0, 0, 1, 2)
+        load_tokens(0, 0, 1)
+        load_tokens(0, 1, 2)
+        load_tables(0, 2)
+        load_rows(0, 1, 0, 2)
+        load_tokens(1, 0, 2)
+        load_tables(2, 4)
+        load_tokens(2, 0, 2)
+        load_tokens(3, 0, 2)
+        load_tables(4, 8)
+        for b in range(1, len(blocks)):
+            for h in range(BLOCK_HEADS):
+                load_rows(b, h, 0, HEAD_ROW_TILES)
+
+        negate_even_sines(0, 2)
+        new_products(0)
+        turn_rows(0, 0, by_scalar)
+        turn_rows(0, 1, by_vector)
+        turn_token(0, by_scalar)
+        turn_token(1, by_vector)
+        quantise_head(0, 0)
+        quantise_tokens(0, 0, 2)
+        multiply_heads(0, 0)
+        turn_rows(0, 2, by_scalar)
+        turn_rows(0, 3, by_scalar)
+        rotate_head(0, 0)
+        add(0, nc.gpsimd, 0, 1)
+        quantise_head(0, 1)
+        multiply_heads(0, 1)
+        turn_token(2, by_scalar)
+        turn_token(3, by_scalar)
+        negate_even_sines(2, 4)
+        rotate_head(0, 1)
+        quantise_tokens(1, 0, 2)
+        multiply_couple(1)
+        add(0, nc.gpsimd, 1, 2)
+        store(0, 0, 2)
+        turn_token(4, by_scalar)
+        turn_token(5, by_scalar)
+        negate_even_sines(4, 8)
+
+        last = len(blocks) * COUPLES - 1
+        for s in range(1, last):
+            b, a = divmod(s, COUPLES)
+            new_products(s)
+            if s == 1:
+                turn_token(6, by_scalar)
+                turn_token(7, by_scalar)
+            if s == 2:
+                turn_rows(1, 0, by_scalar)
+                turn_rows(1, 1, by_scalar)
+            rotate_tile(s, 0)
+            if s in (1, 2):
+                quantise_tokens(s + 1, 0, 2)
+            if s == 3:
+                quantise_block(1)
+            if s + 1 < last:
+                multiply_couple(s + 1)
+            else:
+                multiply_heads(s + 1, 0)
+                multiply_heads(s + 1, 1)
+            if s == 2:
+                turn_rows(1, 2, by_scalar)
+                turn_rows(1, 3, by_scalar)
+            if b > 0 and b + 1 < len(blocks) and a < 2:
+                turn_rows(b + 1, 2 * a, by_scalar)
+                turn_rows(b + 1, 2 * a + 1, by_scalar)
+            rotate_tile(s, 1)
+            if b > 0 and b + 1 < len(blocks) and a == 2:
+                quantise_block(b + 1)
+            add(s, nc.gpsimd, 0, 2)
+            store(s, 0, 2)
+
+        new_products(last)
+        rotate_head(last, 0)
+        rotate_head(last, 1)
+        add(last, nc.vector, 0, 1)
+        store(last, 0, 1)
+        add(last, nc.vector, 1, 2)
+        store(last, 1, 2)

@@ -113,9 +113,7 @@ def tile_nucleusxmultiscaleretention_pa_kernel(
 
         def negate_even_sines(n0, n1):
             even = sin_sb[:, n0:n1, :].rearrange("p n (i e) -> p (n i) e", e=2)[:, :, 0]
-            nc.gpsimd.tensor_scalar(
-                out=even, in0=even, scalar1=-1.0, scalar2=0.0, op0=MULT, op1=ADD
-            )
+            nc.scalar.mul(out=even, in_=even, mul=-1.0)
 
         def turn(rows, grouped_words, copy):
             words = rows.bitcast(F32)
@@ -165,14 +163,14 @@ def tile_nucleusxmultiscaleretention_pa_kernel(
                 in_=grouped_block[b][:],
             )
 
-        def quantise_head(b, h):
-            columns = slice(h * HEAD_DIM, (h + 1) * HEAD_DIM)
+        def quantise_rows(b, j):
+            columns = slice(j * P, (j + 1) * P)
             for g in range(PASSES):
-                first = (g * BLOCK + h * HEAD_DIM) * 4
+                first = (g * BLOCK + j * P) * 4
                 nc.vector.quantize_mx(
                     out=block_codes[b][:, g, columns].bitcast(FP8X4),
                     scales=block_scales[b][:, g, columns],
-                    in_=grouped_block[b][:, first : first + HEAD_DIM * 4],
+                    in_=grouped_block[b][:, first : first + P * 4],
                 )
 
         def product(out, b, n, f0, f1):
@@ -224,6 +222,25 @@ def tile_nucleusxmultiscaleretention_pa_kernel(
                 product(bank[:, t, :], b, a * COUPLE + t, h * HEAD_DIM, (h + 1) * HEAD_DIM)
             state[s, h] = bank
 
+        def multiply_rows(s, j):
+            b, a = divmod(s, COUPLES)
+            bank = block_banks.tile([P, BLOCK_HEADS, HEAD_DIM], F32)
+            for t in range(COUPLE):
+                product(bank[:, 0, t * P : (t + 1) * P], b, a * COUPLE + t, j * P, (j + 1) * P)
+            state[s, "rows", j] = bank
+
+        def rotate_rows(s, j):
+            b, a = divmod(s, COUPLES)
+            h, i = divmod(j, HEAD_ROW_TILES)
+            tiles = slice(a * COUPLE, (a + 1) * COUPLE)
+            columns = slice(i * P, (i + 1) * P)
+            with_cos, with_sin, rotated = state["products", s]
+            rotate(
+                blocks[b][0], state[s, "rows", j][:, 0, :].rearrange("p (t d) -> p t d", t=COUPLE),
+                pairs(cos_sb[:, tiles, columns]), pairs(sin_sb[:, tiles, columns]),
+                with_cos[:, h, :, columns], with_sin[:, h, :, columns],
+            )
+
         def new_products(s):
             with_cos = products.tile([P, BLOCK_HEADS, COUPLE, HEAD_DIM], F32)
             with_sin = products.tile([P, BLOCK_HEADS, COUPLE, HEAD_DIM], F32)
@@ -267,47 +284,53 @@ def tile_nucleusxmultiscaleretention_pa_kernel(
         by_scalar = nc.scalar.copy
         by_vector = nc.vector.tensor_copy
 
+        load_tokens(0, 0, 2)
         load_rows(0, 0, 0, 1)
-        load_rows(0, 0, 1, 2)
-        load_tokens(0, 0, 1)
-        load_tokens(0, 1, 2)
         load_tables(0, 2)
-        load_rows(0, 1, 0, 2)
+        load_rows(0, 0, 1, 2)
+        load_rows(0, 1, 0, 1)
+        load_rows(0, 1, 1, 2)
         load_tokens(1, 0, 2)
         load_tables(2, 4)
         load_tokens(2, 0, 2)
-        load_tokens(3, 0, 2)
         load_tables(4, 8)
+        load_tokens(3, 0, 2)
         for b in range(1, len(blocks)):
             for h in range(BLOCK_HEADS):
                 load_rows(b, h, 0, HEAD_ROW_TILES)
 
-        negate_even_sines(0, 2)
         new_products(0)
-        turn_rows(0, 0, by_scalar)
-        turn_rows(0, 1, by_vector)
-        turn_token(0, by_scalar)
-        turn_token(1, by_vector)
-        quantise_head(0, 0)
+        turn_token(0, by_vector)
+        turn_token(1, by_scalar)
+        negate_even_sines(0, 2)
+        turn_rows(0, 0, by_vector)
         quantise_tokens(0, 0, 2)
-        multiply_heads(0, 0)
+        quantise_rows(0, 0)
+        turn_rows(0, 1, by_scalar)
+        multiply_rows(0, 0)
         turn_rows(0, 2, by_scalar)
+        rotate_rows(0, 0)
+        quantise_rows(0, 1)
+        multiply_rows(0, 1)
+        quantise_rows(0, 2)
         turn_rows(0, 3, by_scalar)
-        rotate_head(0, 0)
-        add(0, nc.gpsimd, 0, 1)
-        quantise_head(0, 1)
-        multiply_heads(0, 1)
+        multiply_rows(0, 2)
         turn_token(2, by_scalar)
         turn_token(3, by_scalar)
         negate_even_sines(2, 4)
-        rotate_head(0, 1)
+        rotate_rows(0, 1)
+        quantise_rows(0, 3)
+        multiply_rows(0, 3)
+        rotate_rows(0, 2)
         quantise_tokens(1, 0, 2)
-        multiply_couple(1)
-        add(0, nc.gpsimd, 1, 2)
-        store(0, 0, 2)
         turn_token(4, by_scalar)
         turn_token(5, by_scalar)
         negate_even_sines(4, 8)
+        multiply_couple(1)
+        rotate_rows(0, 3)
+        add(0, nc.vector, 0, 2)
+        store(0, 0, 2)
+        quantise_tokens(2, 0, 2)
 
         last = len(blocks) * COUPLES - 1
         for s in range(1, last):
@@ -316,27 +339,26 @@ def tile_nucleusxmultiscaleretention_pa_kernel(
             if s == 1:
                 turn_token(6, by_scalar)
                 turn_token(7, by_scalar)
-            if s == 2:
-                turn_rows(1, 0, by_scalar)
-                turn_rows(1, 1, by_scalar)
-            rotate_tile(s, 0)
-            if s in (1, 2):
-                quantise_tokens(s + 1, 0, 2)
-            if s == 3:
-                quantise_block(1)
             if s + 1 < last:
                 multiply_couple(s + 1)
             else:
                 multiply_heads(s + 1, 0)
                 multiply_heads(s + 1, 1)
+            if s == 1:
+                turn_rows(1, 0, by_scalar)
+                turn_rows(1, 1, by_scalar)
             if s == 2:
                 turn_rows(1, 2, by_scalar)
                 turn_rows(1, 3, by_scalar)
             if b > 0 and b + 1 < len(blocks) and a < 2:
                 turn_rows(b + 1, 2 * a, by_scalar)
                 turn_rows(b + 1, 2 * a + 1, by_scalar)
+            rotate_tile(s, 0)
             rotate_tile(s, 1)
-            if b > 0 and b + 1 < len(blocks) and a == 2:
+            if s == 1:
+                quantise_tokens(3, 0, 2)
+            shared = a == 2 and b + 1 < len(blocks)
+            if shared:
                 quantise_block(b + 1)
             add(s, nc.gpsimd, 0, 2)
             store(s, 0, 2)

@@ -284,8 +284,9 @@ def tile_nucleusxmultiscaleretention_pa_kernel(
         by_scalar = nc.scalar.copy
         by_vector = nc.vector.tensor_copy
 
-        load_tokens(0, 0, 2)
+        load_tokens(0, 0, 1)
         load_rows(0, 0, 0, 1)
+        load_tokens(0, 1, 2)
         load_tables(0, 2)
         load_rows(0, 0, 1, 2)
         load_rows(0, 1, 0, 1)
@@ -301,36 +302,36 @@ def tile_nucleusxmultiscaleretention_pa_kernel(
 
         new_products(0)
         turn_token(0, by_vector)
-        turn_token(1, by_scalar)
+        turn_rows(0, 0, by_scalar)
         negate_even_sines(0, 2)
-        turn_rows(0, 0, by_vector)
+        turn_token(1, by_vector)
         quantise_tokens(0, 0, 2)
         quantise_rows(0, 0)
         turn_rows(0, 1, by_scalar)
-        multiply_rows(0, 0)
         turn_rows(0, 2, by_scalar)
+        multiply_rows(0, 0)
         rotate_rows(0, 0)
+        turn_rows(0, 3, by_scalar)
+        turn_token(2, by_scalar)
         quantise_rows(0, 1)
         multiply_rows(0, 1)
         quantise_rows(0, 2)
-        turn_rows(0, 3, by_scalar)
-        multiply_rows(0, 2)
-        turn_token(2, by_scalar)
         turn_token(3, by_scalar)
-        negate_even_sines(2, 4)
+        multiply_rows(0, 2)
         rotate_rows(0, 1)
         quantise_rows(0, 3)
         multiply_rows(0, 3)
         rotate_rows(0, 2)
         quantise_tokens(1, 0, 2)
         turn_token(4, by_scalar)
+        negate_even_sines(2, 4)
         turn_token(5, by_scalar)
         negate_even_sines(4, 8)
         multiply_couple(1)
         rotate_rows(0, 3)
         add(0, nc.vector, 0, 2)
-        store(0, 0, 2)
         quantise_tokens(2, 0, 2)
+        store(0, 0, 2)
 
         last = len(blocks) * COUPLES - 1
         for s in range(1, last):
@@ -345,11 +346,8 @@ def tile_nucleusxmultiscaleretention_pa_kernel(
                 multiply_heads(s + 1, 0)
                 multiply_heads(s + 1, 1)
             if s == 1:
-                turn_rows(1, 0, by_scalar)
-                turn_rows(1, 1, by_scalar)
-            if s == 2:
-                turn_rows(1, 2, by_scalar)
-                turn_rows(1, 3, by_scalar)
+                for j in range(ROW_TILES):
+                    turn_rows(1, j, by_scalar)
             if b > 0 and b + 1 < len(blocks) and a < 2:
                 turn_rows(b + 1, 2 * a, by_scalar)
                 turn_rows(b + 1, 2 * a + 1, by_scalar)
@@ -357,8 +355,7 @@ def tile_nucleusxmultiscaleretention_pa_kernel(
             rotate_tile(s, 1)
             if s == 1:
                 quantise_tokens(3, 0, 2)
-            shared = a == 2 and b + 1 < len(blocks)
-            if shared:
+            if a == 2 and b + 1 < len(blocks):
                 quantise_block(b + 1)
             add(s, nc.gpsimd, 0, 2)
             store(s, 0, 2)

@@ -222,23 +222,24 @@ def tile_nucleusxmultiscaleretention_pa_kernel(
                 product(bank[:, t, :], b, a * COUPLE + t, h * HEAD_DIM, (h + 1) * HEAD_DIM)
             state[s, h] = bank
 
-        def multiply_rows(s, j):
+        def multiply_rows(s, j, t0, t1):
             b, a = divmod(s, COUPLES)
             bank = block_banks.tile([P, BLOCK_HEADS, HEAD_DIM], F32)
-            for t in range(COUPLE):
+            for t in range(t0, t1):
                 product(bank[:, 0, t * P : (t + 1) * P], b, a * COUPLE + t, j * P, (j + 1) * P)
-            state[s, "rows", j] = bank
+            state[s, "rows", j, t0] = bank
 
-        def rotate_rows(s, j):
+        def rotate_rows(s, j, t0, t1):
             b, a = divmod(s, COUPLES)
             h, i = divmod(j, HEAD_ROW_TILES)
-            tiles = slice(a * COUPLE, (a + 1) * COUPLE)
+            tiles = slice(a * COUPLE + t0, a * COUPLE + t1)
             columns = slice(i * P, (i + 1) * P)
             with_cos, with_sin, rotated = state["products", s]
+            bank = state[s, "rows", j, t0][:, 0, :].rearrange("p (t d) -> p t d", t=COUPLE)
             rotate(
-                blocks[b][0], state[s, "rows", j][:, 0, :].rearrange("p (t d) -> p t d", t=COUPLE),
+                blocks[b][0], bank[:, t0:t1, :],
                 pairs(cos_sb[:, tiles, columns]), pairs(sin_sb[:, tiles, columns]),
-                with_cos[:, h, :, columns], with_sin[:, h, :, columns],
+                with_cos[:, h, t0:t1, columns], with_sin[:, h, t0:t1, columns],
             )
 
         def new_products(s):
@@ -272,6 +273,18 @@ def tile_nucleusxmultiscaleretention_pa_kernel(
                 in1=with_sin[:, h0:h1, :, :], op=ADD,
             )
 
+        def add_by_tensor(s, h):
+            with_cos, with_sin, rotated = state["products", s]
+            turned = turn_banks.tile([P, PASSES, HALVES, P], F32)
+            bank = turned[:].rearrange("p g u r -> p (g u r)")
+            for i, product_tile in enumerate((with_cos, with_sin)):
+                nc.tensor.matmul(
+                    out=bank, lhsT=identity[:],
+                    rhs=product_tile[:, h, :, :].rearrange("p t d -> p (t d)"),
+                    start=(i == 0), stop=(i == 1),
+                )
+            nc.scalar.copy(out=rotated[:, h, :, :].rearrange("p t d -> p (t d)"), in_=bank)
+
         def store(s, h0, h1):
             b, a = divmod(s, COUPLES)
             m, c = blocks[b]
@@ -287,11 +300,12 @@ def tile_nucleusxmultiscaleretention_pa_kernel(
         load_tokens(0, 0, 1)
         load_rows(0, 0, 0, 1)
         load_tokens(0, 1, 2)
-        load_tables(0, 2)
         load_rows(0, 0, 1, 2)
         load_rows(0, 1, 0, 1)
+        load_tables(0, 2)
         load_rows(0, 1, 1, 2)
-        load_tokens(1, 0, 2)
+        load_tokens(1, 0, 1)
+        load_tokens(1, 1, 2)
         load_tables(2, 4)
         load_tokens(2, 0, 2)
         load_tables(4, 8)
@@ -303,37 +317,38 @@ def tile_nucleusxmultiscaleretention_pa_kernel(
         new_products(0)
         turn_token(0, by_vector)
         turn_rows(0, 0, by_scalar)
-        negate_even_sines(0, 2)
         turn_token(1, by_vector)
         quantise_tokens(0, 0, 2)
         quantise_rows(0, 0)
         turn_rows(0, 1, by_scalar)
         turn_rows(0, 2, by_scalar)
-        multiply_rows(0, 0)
-        rotate_rows(0, 0)
+        negate_even_sines(0, 2)
+        multiply_rows(0, 0, 0, 2)
+        quantise_rows(0, 1)
+        rotate_rows(0, 0, 0, 2)
+        multiply_rows(0, 1, 0, 2)
         turn_rows(0, 3, by_scalar)
         turn_token(2, by_scalar)
-        quantise_rows(0, 1)
-        multiply_rows(0, 1)
         quantise_rows(0, 2)
+        rotate_rows(0, 1, 0, 2)
+        multiply_rows(0, 2, 0, 2)
         turn_token(3, by_scalar)
-        multiply_rows(0, 2)
-        rotate_rows(0, 1)
         quantise_rows(0, 3)
-        multiply_rows(0, 3)
-        rotate_rows(0, 2)
+        rotate_rows(0, 2, 0, 2)
+        multiply_rows(0, 3, 0, 2)
         quantise_tokens(1, 0, 2)
         turn_token(4, by_scalar)
         negate_even_sines(2, 4)
         turn_token(5, by_scalar)
         negate_even_sines(4, 8)
         multiply_couple(1)
-        rotate_rows(0, 3)
+        rotate_rows(0, 3, 0, 2)
         add(0, nc.vector, 0, 2)
         quantise_tokens(2, 0, 2)
         store(0, 0, 2)
 
         last = len(blocks) * COUPLES - 1
+        by_tensor = {(COUPLES + 1, 1), (2 * COUPLES + 1, 1), (last - 1, 1)}
         for s in range(1, last):
             b, a = divmod(s, COUPLES)
             new_products(s)
@@ -351,16 +366,26 @@ def tile_nucleusxmultiscaleretention_pa_kernel(
             if b > 0 and b + 1 < len(blocks) and a < 2:
                 turn_rows(b + 1, 2 * a, by_scalar)
                 turn_rows(b + 1, 2 * a + 1, by_scalar)
+            for h in range(BLOCK_HEADS):
+                if (s - 1, h) in by_tensor:
+                    add_by_tensor(s - 1, h)
+                    store(s - 1, h, h + 1)
             rotate_tile(s, 0)
             rotate_tile(s, 1)
             if s == 1:
                 quantise_tokens(3, 0, 2)
             if a == 2 and b + 1 < len(blocks):
                 quantise_block(b + 1)
-            add(s, nc.gpsimd, 0, 2)
-            store(s, 0, 2)
+            heads = [h for h in range(BLOCK_HEADS) if (s, h) not in by_tensor]
+            if heads:
+                add(s, nc.gpsimd, heads[0], heads[-1] + 1)
+                store(s, heads[0], heads[-1] + 1)
 
         new_products(last)
+        for h in range(BLOCK_HEADS):
+            if (last - 1, h) in by_tensor:
+                add_by_tensor(last - 1, h)
+                store(last - 1, h, h + 1)
         rotate_head(last, 0)
         rotate_head(last, 1)
         add(last, nc.vector, 0, 1)

@@ -54,6 +54,7 @@ def tile_nucleusxmultiscaleretention_pa_kernel(
         keep = ctx.enter_context(tc.tile_pool(name="keep", bufs=1))
         stage_tokens = ctx.enter_context(tc.tile_pool(name="stage_tokens", bufs=3))
         stage_block = ctx.enter_context(tc.tile_pool(name="stage_block", bufs=2))
+        stage_rows = ctx.enter_context(tc.tile_pool(name="stage_rows", bufs=ROW_TILES))
         products = ctx.enter_context(tc.tile_pool(name="products", bufs=4))
         results = ctx.enter_context(tc.tile_pool(name="results", bufs=6))
         turn_banks = ctx.enter_context(tc.psum_pool(name="turn_banks", bufs=4))
@@ -126,6 +127,7 @@ def tile_nucleusxmultiscaleretention_pa_kernel(
 
         grouped_tokens = {}
         grouped_block = {}
+        grouped_rows = {}
 
         def turn_token(n, copy):
             a, t = divmod(n, COUPLE)
@@ -146,6 +148,13 @@ def tile_nucleusxmultiscaleretention_pa_kernel(
                 in_=grouped_tokens[a][:, t0:t1, :].rearrange("p t w -> p (t w)"),
             )
 
+        def turn_first_rows(j, copy):
+            grouped = stage_rows.tile([P, PASSES * P * 4], BF16, align_bytes=64)
+            grouped_rows[j] = grouped
+            h, i = divmod(j, HEAD_ROW_TILES)
+            view = grouped[:].bitcast(F32).rearrange("p (g r u) -> p g r u", g=PASSES, u=HALVES)
+            turn(raw_block[0][h][:, i, :], view, copy)
+
         def turn_rows(b, j, copy):
             if j == 0:
                 grouped = stage_block.tile([P, PASSES * BLOCK * 4], BF16, align_bytes=64)
@@ -163,14 +172,13 @@ def tile_nucleusxmultiscaleretention_pa_kernel(
                 in_=grouped_block[b][:],
             )
 
-        def quantise_rows(b, j):
+        def quantise_first_rows(j):
             columns = slice(j * P, (j + 1) * P)
             for g in range(PASSES):
-                first = (g * BLOCK + j * P) * 4
                 nc.vector.quantize_mx(
-                    out=block_codes[b][:, g, columns].bitcast(FP8X4),
-                    scales=block_scales[b][:, g, columns],
-                    in_=grouped_block[b][:, first : first + P * 4],
+                    out=block_codes[0][:, g, columns].bitcast(FP8X4),
+                    scales=block_scales[0][:, g, columns],
+                    in_=grouped_rows[j][:, g * P * 4 : (g + 1) * P * 4],
                 )
 
         def product(out, b, n, f0, f1):
@@ -316,24 +324,24 @@ def tile_nucleusxmultiscaleretention_pa_kernel(
 
         new_products(0)
         turn_token(0, by_vector)
-        turn_rows(0, 0, by_scalar)
+        turn_first_rows(0, by_scalar)
         turn_token(1, by_vector)
         quantise_tokens(0, 0, 2)
-        quantise_rows(0, 0)
-        turn_rows(0, 1, by_scalar)
-        turn_rows(0, 2, by_scalar)
+        quantise_first_rows(0)
+        turn_first_rows(1, by_scalar)
+        turn_first_rows(2, by_scalar)
         negate_even_sines(0, 2)
         multiply_rows(0, 0, 0, 2)
-        quantise_rows(0, 1)
+        quantise_first_rows(1)
         rotate_rows(0, 0, 0, 2)
         multiply_rows(0, 1, 0, 2)
-        turn_rows(0, 3, by_scalar)
+        turn_first_rows(3, by_scalar)
         turn_token(2, by_scalar)
-        quantise_rows(0, 2)
+        quantise_first_rows(2)
         rotate_rows(0, 1, 0, 2)
         multiply_rows(0, 2, 0, 2)
         turn_token(3, by_scalar)
-        quantise_rows(0, 3)
+        quantise_first_rows(3)
         rotate_rows(0, 2, 0, 2)
         multiply_rows(0, 3, 0, 2)
         quantise_tokens(1, 0, 2)

@@ -45,9 +45,12 @@ def tile_nucleusxmultiscaleretention_pa_kernel(
     ]
     cos_rows = cos.rearrange("(p n) d -> p n d", n=TOKEN_TILES)
     sin_rows = sin.rearrange("(p n) d -> p n d", n=TOKEN_TILES)
-    out_rows = [
+    couple_rows = [
         o[0].rearrange("(c h) (p a t) d -> c a p h (t d)", c=BLOCKS, a=COUPLES, t=COUPLE)
         for o in (out_0, out_1)
+    ]
+    head_rows = [
+        o[0].rearrange("h (p a t) d -> h p a (t d)", a=COUPLES, t=COUPLE) for o in (out_0, out_1)
     ]
 
     with ExitStack() as ctx:
@@ -86,11 +89,11 @@ def tile_nucleusxmultiscaleretention_pa_kernel(
             for a in range(COUPLES)
         ]
         block_codes = [
-            keep.tile([P, PASSES, BLOCK], U32, name="block_codes%d" % b, align_bytes=64)
+            keep.tile([P, BLOCK_HEADS, PASSES * HEAD_DIM], U32, name="block_codes%d" % b, align_bytes=64)
             for b in range(len(blocks))
         ]
         block_scales = [
-            keep.tile([P, PASSES, BLOCK], U8, name="block_scales%d" % b, align_bytes=64)
+            keep.tile([P, BLOCK_HEADS, PASSES * HEAD_DIM], U8, name="block_scales%d" % b, align_bytes=64)
             for b in range(len(blocks))
         ]
 
@@ -155,42 +158,45 @@ def tile_nucleusxmultiscaleretention_pa_kernel(
             view = grouped[:].bitcast(F32).rearrange("p (g r u) -> p g r u", g=PASSES, u=HALVES)
             turn(raw_block[0][h][:, i, :], view, copy)
 
-        def turn_rows(b, j, copy):
-            if j == 0:
-                grouped = stage_block.tile([P, PASSES * BLOCK * 4], BF16, align_bytes=64)
+        def turn_rows(b, h, i, copy):
+            if (h, i) == (0, 0):
+                grouped = stage_block.tile(
+                    [P, BLOCK_HEADS, PASSES * HEAD_DIM * 4], BF16, align_bytes=64
+                )
                 grouped_block[b] = grouped
-            words = grouped_block[b][:].bitcast(F32).rearrange(
-                "p (g j r u) -> p g j r u", g=PASSES, j=ROW_TILES, u=HALVES
+            words = grouped_block[b][:, h, :].bitcast(F32).rearrange(
+                "p (g j r u) -> p g j r u", g=PASSES, j=HEAD_ROW_TILES, u=HALVES
             )
-            h, i = divmod(j, HEAD_ROW_TILES)
-            turn(raw_block[b][h][:, i, :], words[:, :, j, :, :], copy)
+            turn(raw_block[b][h][:, i, :], words[:, :, i, :, :], copy)
 
-        def quantise_block(b):
+        def quantise_heads(b, h0, h1):
             nc.vector.quantize_mx(
-                out=block_codes[b][:].rearrange("p g f -> p (g f)").bitcast(FP8X4),
-                scales=block_scales[b][:].rearrange("p g f -> p (g f)"),
-                in_=grouped_block[b][:],
+                out=block_codes[b][:, h0:h1, :].rearrange("p h w -> p (h w)").bitcast(FP8X4),
+                scales=block_scales[b][:, h0:h1, :].rearrange("p h w -> p (h w)"),
+                in_=grouped_block[b][:, h0:h1, :].rearrange("p h w -> p (h w)"),
             )
 
         def quantise_first_rows(j):
-            columns = slice(j * P, (j + 1) * P)
+            h, i = divmod(j, HEAD_ROW_TILES)
             for g in range(PASSES):
+                columns = slice(g * HEAD_DIM + i * P, g * HEAD_DIM + (i + 1) * P)
                 nc.vector.quantize_mx(
-                    out=block_codes[0][:, g, columns].bitcast(FP8X4),
-                    scales=block_scales[0][:, g, columns],
+                    out=block_codes[0][:, h, columns].bitcast(FP8X4),
+                    scales=block_scales[0][:, h, columns],
                     in_=grouped_rows[j][:, g * P * 4 : (g + 1) * P * 4],
                 )
 
-        def product(out, b, n, f0, f1):
+        def product(out, b, n, h, f0, f1):
             a, t = divmod(n, COUPLE)
             for g in range(PASSES):
                 tokens = slice(g * P, (g + 1) * P)
+                features = slice(g * HEAD_DIM + f0, g * HEAD_DIM + f1)
                 nc.tensor.matmul_mx(
                     out=out,
                     lhsT=token_codes[a][:, t, tokens].bitcast(FP8X4),
                     lhsT_scale=token_scales[a][:, t, tokens],
-                    rhs=block_codes[b][:, g, f0:f1].bitcast(FP8X4),
-                    rhs_scale=block_scales[b][:, g, f0:f1],
+                    rhs=block_codes[b][:, h, features].bitcast(FP8X4),
+                    rhs_scale=block_scales[b][:, h, features],
                     start=(g == 0),
                     stop=(g == PASSES - 1),
                 )
@@ -214,27 +220,29 @@ def tile_nucleusxmultiscaleretention_pa_kernel(
 
         state = {}
 
-        def multiply_couple(s):
-            b, a = divmod(s, COUPLES)
+        def multiply(s):
             banks = []
-            for t in range(COUPLE):
-                bank = block_banks.tile([P, BLOCK_HEADS, HEAD_DIM], F32)
-                product(bank[:].rearrange("p h d -> p (h d)"), b, a * COUPLE + t, 0, BLOCK)
+            for part in range(2):
+                bank = block_banks.tile([P, 2, HEAD_DIM], F32)
+                for i in range(2):
+                    if s // COUPLES != 1:
+                        b, a = divmod(s, COUPLES)
+                        product(bank[:, i, :], b, a * COUPLE + part, i, 0, HEAD_DIM)
+                    else:
+                        b, h, q = divide(s)
+                        product(bank[:, i, :], b, (2 * q + part) * COUPLE + i, h, 0, HEAD_DIM)
                 banks.append(bank)
             state[s] = banks
 
-        def multiply_heads(s, h):
-            b, a = divmod(s, COUPLES)
-            bank = block_banks.tile([P, BLOCK_HEADS, HEAD_DIM], F32)
-            for t in range(COUPLE):
-                product(bank[:, t, :], b, a * COUPLE + t, h * HEAD_DIM, (h + 1) * HEAD_DIM)
-            state[s, h] = bank
+        def divide(s):
+            return s // COUPLES, s % COUPLES // 2, s % 2
 
         def multiply_rows(s, j, t0, t1):
             b, a = divmod(s, COUPLES)
+            h, i = divmod(j, HEAD_ROW_TILES)
             bank = block_banks.tile([P, BLOCK_HEADS, HEAD_DIM], F32)
             for t in range(t0, t1):
-                product(bank[:, 0, t * P : (t + 1) * P], b, a * COUPLE + t, j * P, (j + 1) * P)
+                product(bank[:, 0, t * P : (t + 1) * P], b, a * COUPLE + t, h, i * P, (i + 1) * P)
             state[s, "rows", j, t0] = bank
 
         def rotate_rows(s, j, t0, t1):
@@ -256,23 +264,23 @@ def tile_nucleusxmultiscaleretention_pa_kernel(
             rotated = results.tile([P, BLOCK_HEADS, COUPLE, HEAD_DIM], F32)
             state["products", s] = (with_cos, with_sin, rotated)
 
-        def rotate_tile(s, t):
-            b, a = divmod(s, COUPLES)
-            n = a * COUPLE + t
+        def rotate_part(s, part):
             with_cos, with_sin, rotated = state["products", s]
-            rotate(
-                blocks[b][0], state[s][t][:], table_for_heads(cos_sb, n), table_for_heads(sin_sb, n),
-                with_cos[:, :, t, :], with_sin[:, :, t, :],
-            )
-
-        def rotate_head(s, h):
-            b, a = divmod(s, COUPLES)
-            tiles = slice(a * COUPLE, (a + 1) * COUPLE)
-            with_cos, with_sin, rotated = state["products", s]
-            rotate(
-                blocks[b][0], state[s, h][:], pairs(cos_sb[:, tiles, :]), pairs(sin_sb[:, tiles, :]),
-                with_cos[:, h, :, :], with_sin[:, h, :, :],
-            )
+            if s // COUPLES != 1:
+                b, a = divmod(s, COUPLES)
+                n = a * COUPLE + part
+                rotate(
+                    blocks[b][0], state[s][part][:], table_for_heads(cos_sb, n),
+                    table_for_heads(sin_sb, n), with_cos[:, :, part, :], with_sin[:, :, part, :],
+                )
+            else:
+                b, h, q = divide(s)
+                first = (2 * q + part) * COUPLE
+                tiles = slice(first, first + COUPLE)
+                rotate(
+                    blocks[b][0], state[s][part][:], pairs(cos_sb[:, tiles, :]),
+                    pairs(sin_sb[:, tiles, :]), with_cos[:, part, :, :], with_sin[:, part, :, :],
+                )
 
         def add(s, engine, h0, h1):
             with_cos, with_sin, rotated = state["products", s]
@@ -294,12 +302,17 @@ def tile_nucleusxmultiscaleretention_pa_kernel(
             nc.scalar.copy(out=rotated[:, h, :, :].rearrange("p t d -> p (t d)"), in_=bank)
 
         def store(s, h0, h1):
-            b, a = divmod(s, COUPLES)
-            m, c = blocks[b]
+            if s // COUPLES != 1:
+                b, a = divmod(s, COUPLES)
+                m, c = blocks[b]
+                rows = couple_rows[m][c, a][:, h0:h1, :]
+            else:
+                b, h, q = divide(s)
+                m, c = blocks[b]
+                rows = head_rows[m][c * BLOCK_HEADS + h][:, 2 * q + h0 : 2 * q + h1, :]
             rotated = state["products", s][2]
             nc.sync.dma_start(
-                out=out_rows[m][c, a][:, h0:h1, :],
-                in_=rotated[:, h0:h1, :, :].rearrange("p h t d -> p h (t d)"),
+                out=rows, in_=rotated[:, h0:h1, :, :].rearrange("p h t d -> p h (t d)")
             )
 
         by_scalar = nc.scalar.copy
@@ -333,69 +346,68 @@ def tile_nucleusxmultiscaleretention_pa_kernel(
         negate_even_sines(0, 2)
         multiply_rows(0, 0, 0, 2)
         quantise_first_rows(1)
-        rotate_rows(0, 0, 0, 2)
-        multiply_rows(0, 1, 0, 2)
         turn_first_rows(3, by_scalar)
-        turn_token(2, by_scalar)
+        multiply_rows(0, 1, 0, 2)
+        rotate_rows(0, 0, 0, 2)
         quantise_first_rows(2)
-        rotate_rows(0, 1, 0, 2)
-        multiply_rows(0, 2, 0, 2)
+        turn_token(2, by_scalar)
         turn_token(3, by_scalar)
+        multiply_rows(0, 2, 0, 2)
+        rotate_rows(0, 1, 0, 2)
         quantise_first_rows(3)
-        rotate_rows(0, 2, 0, 2)
-        multiply_rows(0, 3, 0, 2)
-        quantise_tokens(1, 0, 2)
         turn_token(4, by_scalar)
-        negate_even_sines(2, 4)
         turn_token(5, by_scalar)
+        multiply_rows(0, 3, 0, 2)
+        negate_even_sines(2, 4)
         negate_even_sines(4, 8)
-        multiply_couple(1)
+        rotate_rows(0, 2, 0, 2)
+        quantise_tokens(1, 0, 2)
+        multiply(1)
         rotate_rows(0, 3, 0, 2)
-        add(0, nc.vector, 0, 2)
         quantise_tokens(2, 0, 2)
+        add(0, nc.gpsimd, 0, 2)
         store(0, 0, 2)
 
         last = len(blocks) * COUPLES - 1
         by_tensor = {(COUPLES + 1, 1), (2 * COUPLES + 1, 1), (last - 1, 1)}
         for s in range(1, last):
-            b, a = divmod(s, COUPLES)
             new_products(s)
             if s == 1:
                 turn_token(6, by_scalar)
                 turn_token(7, by_scalar)
-            if s + 1 < last:
-                multiply_couple(s + 1)
-            else:
-                multiply_heads(s + 1, 0)
-                multiply_heads(s + 1, 1)
-            if s == 1:
-                for j in range(ROW_TILES):
-                    turn_rows(1, j, by_scalar)
+            multiply(s + 1)
+            b, a = divmod(s, COUPLES)
+            if b == 0 and a > 0 and a < 3:
+                for i in range(HEAD_ROW_TILES):
+                    turn_rows(1, a - 1, i, by_scalar)
             if b > 0 and b + 1 < len(blocks) and a < 2:
-                turn_rows(b + 1, 2 * a, by_scalar)
-                turn_rows(b + 1, 2 * a + 1, by_scalar)
-            for h in range(BLOCK_HEADS):
+                for i in range(HEAD_ROW_TILES):
+                    turn_rows(b + 1, a, i, by_scalar)
+            for h in range(2):
                 if (s - 1, h) in by_tensor:
                     add_by_tensor(s - 1, h)
                     store(s - 1, h, h + 1)
-            rotate_tile(s, 0)
-            rotate_tile(s, 1)
+            rotate_part(s, 0)
+            rotate_part(s, 1)
             if s == 1:
                 quantise_tokens(3, 0, 2)
-            if a == 2 and b + 1 < len(blocks):
-                quantise_block(b + 1)
-            heads = [h for h in range(BLOCK_HEADS) if (s, h) not in by_tensor]
-            if heads:
-                add(s, nc.gpsimd, heads[0], heads[-1] + 1)
-                store(s, heads[0], heads[-1] + 1)
+            if s == 2:
+                quantise_heads(1, 0, 1)
+            if s == 3:
+                quantise_heads(1, 1, 2)
+            if b > 0 and b + 1 < len(blocks) and a == 2:
+                quantise_heads(b + 1, 0, 2)
+            heads = [h for h in range(2) if (s, h) not in by_tensor]
+            add(s, nc.gpsimd, heads[0], heads[-1] + 1)
+            store(s, heads[0], heads[-1] + 1)
 
         new_products(last)
-        for h in range(BLOCK_HEADS):
+        for h in range(2):
             if (last - 1, h) in by_tensor:
                 add_by_tensor(last - 1, h)
                 store(last - 1, h, h + 1)
-        rotate_head(last, 0)
-        rotate_head(last, 1)
+        rotate_part(last, 0)
+        rotate_part(last, 1)
         add(last, nc.vector, 0, 1)
         store(last, 0, 1)
         add(last, nc.vector, 1, 2)

@@ -327,28 +327,31 @@ def tile_nucleusxmultiscaleretention_pa_kernel(
         load_rows(0, 1, 1, 2)
         load_tokens(1, 0, 1)
         load_tokens(1, 1, 2)
-        load_tables(2, 4)
         load_tokens(2, 0, 2)
-        load_tables(4, 8)
+        load_tables(2, 4)
         load_tokens(3, 0, 2)
+        load_tables(4, 8)
         for b in range(1, len(blocks)):
             for h in range(BLOCK_HEADS):
                 load_rows(b, h, 0, HEAD_ROW_TILES)
 
         new_products(0)
         turn_token(0, by_vector)
-        turn_first_rows(0, by_scalar)
-        turn_token(1, by_vector)
-        quantise_tokens(0, 0, 2)
+        turn_first_rows(0, by_vector)
         quantise_first_rows(0)
+        quantise_tokens(0, 0, 1)
+        turn_token(1, by_scalar)
         turn_first_rows(1, by_scalar)
-        turn_first_rows(2, by_scalar)
         negate_even_sines(0, 2)
-        multiply_rows(0, 0, 0, 2)
+        turn_first_rows(2, by_scalar)
+        multiply_rows(0, 0, 0, 1)
+        quantise_tokens(0, 1, 2)
+        multiply_rows(0, 0, 1, 2)
         quantise_first_rows(1)
+        rotate_rows(0, 0, 0, 1)
+        rotate_rows(0, 0, 1, 2)
         turn_first_rows(3, by_scalar)
         multiply_rows(0, 1, 0, 2)
-        rotate_rows(0, 0, 0, 2)
         quantise_first_rows(2)
         turn_token(2, by_scalar)
         turn_token(3, by_scalar)
@@ -359,10 +362,12 @@ def tile_nucleusxmultiscaleretention_pa_kernel(
         turn_token(5, by_scalar)
         multiply_rows(0, 3, 0, 2)
         negate_even_sines(2, 4)
-        negate_even_sines(4, 8)
         rotate_rows(0, 2, 0, 2)
         quantise_tokens(1, 0, 2)
+        turn_token(6, by_scalar)
         multiply(1)
+        turn_token(7, by_scalar)
+        negate_even_sines(4, 8)
         rotate_rows(0, 3, 0, 2)
         quantise_tokens(2, 0, 2)
         add(0, nc.gpsimd, 0, 2)
@@ -372,9 +377,6 @@ def tile_nucleusxmultiscaleretention_pa_kernel(
         by_tensor = {(COUPLES + 1, 1), (2 * COUPLES + 1, 1), (last - 1, 1)}
         for s in range(1, last):
             new_products(s)
-            if s == 1:
-                turn_token(6, by_scalar)
-                turn_token(7, by_scalar)
             multiply(s + 1)
             b, a = divmod(s, COUPLES)
             if b == 0 and a > 0 and a < 3:

@@ -59,6 +59,7 @@ def tile_nucleusxmultiscaleretention_pa_kernel(
         stage_block = ctx.enter_context(tc.tile_pool(name="stage_block", bufs=2))
         stage_rows = ctx.enter_context(tc.tile_pool(name="stage_rows", bufs=ROW_TILES))
         products = ctx.enter_context(tc.tile_pool(name="products", bufs=4))
+        copies = ctx.enter_context(tc.tile_pool(name="copies", bufs=2))
         results = ctx.enter_context(tc.tile_pool(name="results", bufs=6))
         turn_banks = ctx.enter_context(tc.psum_pool(name="turn_banks", bufs=4))
         block_banks = ctx.enter_context(tc.psum_pool(name="block_banks", bufs=4))
@@ -264,6 +265,22 @@ def tile_nucleusxmultiscaleretention_pa_kernel(
             rotated = results.tile([P, BLOCK_HEADS, COUPLE, HEAD_DIM], F32)
             state["products", s] = (with_cos, with_sin, rotated)
 
+        def rotate_part_shared(s, part):
+            b, a = divmod(s, COUPLES)
+            n = a * COUPLE + part
+            with_cos, with_sin, rotated = state["products", s]
+            bank = state[s][part]
+            copied = copies.tile([P, BLOCK_HEADS, HEAD_DIM], F32)
+            nc.scalar.mul(out=copied[:], in_=bank[:], mul=scalings[blocks[b][0]])
+            nc.gpsimd.tensor_tensor(
+                out=pairs(with_sin[:, :, part, :]), in0=pairs(copied[:])[:, :, :, ::-1],
+                in1=table_for_heads(sin_sb, n), op=MULT,
+            )
+            nc.vector.scalar_tensor_tensor(
+                out=pairs(with_cos[:, :, part, :]), in0=pairs(bank[:]), scalar=scalings[blocks[b][0]],
+                in1=table_for_heads(cos_sb, n), op0=MULT, op1=MULT,
+            )
+
         def rotate_part(s, part):
             with_cos, with_sin, rotated = state["products", s]
             if s // COUPLES != 1:
@@ -374,7 +391,7 @@ def tile_nucleusxmultiscaleretention_pa_kernel(
         store(0, 0, 2)
 
         last = len(blocks) * COUPLES - 1
-        by_tensor = {(COUPLES + 1, 1), (2 * COUPLES + 1, 1), (last - 1, 1)}
+        by_tensor = {(COUPLES + 1, 1), (2 * COUPLES + 1, 1), (3 * COUPLES, 1), (last - 1, 1)}
         for s in range(1, last):
             new_products(s)
             multiply(s + 1)
@@ -389,8 +406,8 @@ def tile_nucleusxmultiscaleretention_pa_kernel(
                 if (s - 1, h) in by_tensor:
                     add_by_tensor(s - 1, h)
                     store(s - 1, h, h + 1)
-            rotate_part(s, 0)
-            rotate_part(s, 1)
+            for part in range(2):
+                (rotate_part_shared if (s, part) in ((3 * COUPLES - 1, 1),) else rotate_part)(s, part)
             if s == 1:
                 quantise_tokens(3, 0, 2)
             if s == 2:

from contextlib import ExitStack

import concourse.mybir as mybir
from concourse.masks import make_identity

F32 = mybir.dt.float32
BF16 = mybir.dt.bfloat16
U32 = mybir.dt.uint32
U8 = mybir.dt.uint8
FP8X4 = mybir.dt.float8_e4m3fn_x4
MULT = mybir.AluOpType.mult
ADD = mybir.AluOpType.add

P = 128
TOKENS = 1024
K = 1024
HEADS = 4
HEAD_DIM = 256
BLOCK = 512
BLOCK_HEADS = BLOCK // HEAD_DIM
BLOCKS = HEADS * HEAD_DIM // BLOCK
ROW_TILES = BLOCK // P
HEAD_ROW_TILES = HEAD_DIM // P
K_PASS = 4 * P
PASSES = K // K_PASS
HALVES = 2
TOKEN_TILES = TOKENS // P
COUPLE = 2
COUPLES = TOKEN_TILES // COUPLE
K_SCALING = HEAD_DIM ** -0.5

FLOPS = 2 * TOKENS * K * (2 * HEADS * HEAD_DIM)


def tile_nucleusxmultiscaleretention_pa_kernel(
    tc, hidden_states, wq, wk, sin, cos, out_0, out_1
):
    nc = tc.nc
    scalings = [1.0, K_SCALING]
    blocks = [(m, c) for m in range(2) for c in range(BLOCKS)]

    token_rows = hidden_states[0].rearrange("(p n) k -> p n k", n=TOKEN_TILES)
    weight_rows = [
        w.rearrange("(c j r) k -> c r j k", c=BLOCKS, j=ROW_TILES) for w in (wq, wk)
    ]
    cos_rows = cos.rearrange("(p n) d -> p n d", n=TOKEN_TILES)
    sin_rows = sin.rearrange("(p n) d -> p n d", n=TOKEN_TILES)
    couple_rows = [
        o[0].rearrange("(c h) (p a t) d -> c a p h (t d)", c=BLOCKS, a=COUPLES, t=COUPLE)
        for o in (out_0, out_1)
    ]
    head_rows = [
        o[0].rearrange("h (p a t) d -> h p a (t d)", a=COUPLES, t=COUPLE) for o in (out_0, out_1)
    ]

    with ExitStack() as ctx:
        keep = ctx.enter_context(tc.tile_pool(name="keep", bufs=1))
        stage_tokens = ctx.enter_context(tc.tile_pool(name="stage_tokens", bufs=3))
        stage_block = ctx.enter_context(tc.tile_pool(name="stage_block", bufs=2))
        stage_rows = ctx.enter_context(tc.tile_pool(name="stage_rows", bufs=ROW_TILES))
        products = ctx.enter_context(tc.tile_pool(name="products", bufs=4))
        copies = ctx.enter_context(tc.tile_pool(name="copies", bufs=2))
        results = ctx.enter_context(tc.tile_pool(name="results", bufs=6))
        turn_banks = ctx.enter_context(tc.psum_pool(name="turn_banks", bufs=4))
        block_banks = ctx.enter_context(tc.psum_pool(name="block_banks", bufs=4))
        ctx.enter_context(tc.manual_schedule())

        identity = keep.tile([P, P], F32)
        make_identity(nc, identity[:])

        raw_tokens = [
            keep.tile([P, COUPLE, K], BF16, name="raw_tokens%d" % a) for a in range(COUPLES)
        ]
        raw_block = [
            [
                keep.tile([P, HEAD_ROW_TILES, K], BF16, name="raw_w%d_%d" % (b, h))
                for h in range(BLOCK_HEADS)
            ]
            for b in range(len(blocks))
        ]
        cos_sb = keep.tile([P, TOKEN_TILES, HEAD_DIM], BF16)
        sin_sb = keep.tile([P, TOKEN_TILES, HEAD_DIM], BF16)

        token_codes = [
            keep.tile([P, COUPLE, PASSES * P], U32, name="token_codes%d" % a, align_bytes=64)
            for a in range(COUPLES)
        ]
        token_scales = [
            keep.tile([P, COUPLE, PASSES * P], U8, name="token_scales%d" % a, align_bytes=64)
            for a in range(COUPLES)
        ]
        block_codes = [
            keep.tile([P, BLOCK_HEADS, PASSES * HEAD_DIM], U32, name="block_codes%d" % b, align_bytes=64)
            for b in range(len(blocks))
        ]
        block_scales = [
            keep.tile([P, BLOCK_HEADS, PASSES * HEAD_DIM], U8, name="block_scales%d" % b, align_bytes=64)
            for b in range(len(blocks))
        ]

        def load_tokens(a, t0, t1):
            nc.sync.dma_start(
                out=raw_tokens[a][:, t0:t1, :],
                in_=token_rows[:, a * COUPLE + t0 : a * COUPLE + t1, :],
            )

        def load_rows(b, h, j0, j1):
            m, c = blocks[b]
            first = h * HEAD_ROW_TILES
            nc.sync.dma_start(
                out=raw_block[b][h][:, j0:j1, :],
                in_=weight_rows[m][c, :, first + j0 : first + j1, :],
            )

        def load_tables(n0, n1):
            nc.sync.dma_start(out=cos_sb[:, n0:n1, :], in_=cos_rows[:, n0:n1, :])
            nc.sync.dma_start(out=sin_sb[:, n0:n1, :], in_=sin_rows[:, n0:n1, :])

        def negate_even_sines(n0, n1):
            even = sin_sb[:, n0:n1, :].rearrange("p n (i e) -> p (n i) e", e=2)[:, :, 0]
            nc.scalar.mul(out=even, in_=even, mul=-1.0)

        def turn(rows, grouped_words, copy):
            words = rows.bitcast(F32)
            turned = turn_banks.tile([P, PASSES, HALVES, P], F32)
            for g in range(PASSES):
                for u in range(HALVES):
                    every_second = words[:, g * HALVES * P + u : (g + 1) * HALVES * P : HALVES]
                    nc.tensor.transpose(turned[:, g, u, :], every_second, identity[:])
            copy(out=grouped_words, in_=turned[:].rearrange("p g u r -> p g r u"))

        grouped_tokens = {}
        grouped_block = {}
        grouped_rows = {}

        def turn_token(n, copy):
            a, t = divmod(n, COUPLE)
            if t == 0:
                grouped_couple = stage_tokens.tile([P, COUPLE, PASSES * P * 4], BF16, align_bytes=64)
                grouped_tokens[a] = grouped_couple
            view = grouped_tokens[a][:, t, :].bitcast(F32)
            turn(
                raw_tokens[a][:, t, :],
                view.rearrange("p (g r u) -> p g r u", g=PASSES, u=HALVES),
                copy,
            )

        def quantise_tokens(a, t0, t1):
            nc.vector.quantize_mx(
                out=token_codes[a][:, t0:t1, :].rearrange("p t w -> p (t w)").bitcast(FP8X4),
                scales=token_scales[a][:, t0:t1, :].rearrange("p t w -> p (t w)"),
                in_=grouped_tokens[a][:, t0:t1, :].rearrange("p t w -> p (t w)"),
            )

        def turn_first_rows(j, copy):
            grouped = stage_rows.tile([P, PASSES * P * 4], BF16, align_bytes=64)
            grouped_rows[j] = grouped
            h, i = divmod(j, HEAD_ROW_TILES)
            view = grouped[:].bitcast(F32).rearrange("p (g r u) -> p g r u", g=PASSES, u=HALVES)
            turn(raw_block[0][h][:, i, :], view, copy)

        def turn_rows(b, h, i, copy):
            if (h, i) == (0, 0):
                grouped = stage_block.tile(
                    [P, BLOCK_HEADS, PASSES * HEAD_DIM * 4], BF16, align_bytes=64
                )
                grouped_block[b] = grouped
            words = grouped_block[b][:, h, :].bitcast(F32).rearrange(
                "p (g j r u) -> p g j r u", g=PASSES, j=HEAD_ROW_TILES, u=HALVES
            )
            turn(raw_block[b][h][:, i, :], words[:, :, i, :, :], copy)

        def quantise_heads(b, h0, h1):
            nc.vector.quantize_mx(
                out=block_codes[b][:, h0:h1, :].rearrange("p h w -> p (h w)").bitcast(FP8X4),
                scales=block_scales[b][:, h0:h1, :].rearrange("p h w -> p (h w)"),
                in_=grouped_block[b][:, h0:h1, :].rearrange("p h w -> p (h w)"),
            )

        def quantise_first_rows(j):
            h, i = divmod(j, HEAD_ROW_TILES)
            for g in range(PASSES):
                columns = slice(g * HEAD_DIM + i * P, g * HEAD_DIM + (i + 1) * P)
                nc.vector.quantize_mx(
                    out=block_codes[0][:, h, columns].bitcast(FP8X4),
                    scales=block_scales[0][:, h, columns],
                    in_=grouped_rows[j][:, g * P * 4 : (g + 1) * P * 4],
                )

        def product(out, b, n, h, f0, f1):
            a, t = divmod(n, COUPLE)
            for g in range(PASSES):
                tokens = slice(g * P, (g + 1) * P)
                features = slice(g * HEAD_DIM + f0, g * HEAD_DIM + f1)
                nc.tensor.matmul_mx(
                    out=out,
                    lhsT=token_codes[a][:, t, tokens].bitcast(FP8X4),
                    lhsT_scale=token_scales[a][:, t, tokens],
                    rhs=block_codes[b][:, h, features].bitcast(FP8X4),
                    rhs_scale=block_scales[b][:, h, features],
                    start=(g == 0),
                    stop=(g == PASSES - 1),
                )

        def pairs(view):
            return view.rearrange("p x (i e) -> p x i e", e=2)

        def rotate(m, bank, cos_view, sin_view, with_cos, with_sin):
            nc.vector.scalar_tensor_tensor(
                out=pairs(with_cos), in0=pairs(bank), scalar=scalings[m], in1=cos_view,
                op0=MULT, op1=MULT,
            )
            nc.vector.scalar_tensor_tensor(
                out=pairs(with_sin), in0=pairs(bank)[:, :, :, ::-1], scalar=scalings[m],
                in1=sin_view, op0=MULT, op1=MULT,
            )

        def table_for_heads(table, n):
            one_head = table[:, n, :].rearrange("p (i e) -> p i e", e=2)
            return one_head.unsqueeze(1).to_broadcast([P, BLOCK_HEADS, HEAD_DIM // 2, 2])

        state = {}

        def multiply(s):
            banks = []
            for part in range(2):
                bank = block_banks.tile([P, 2, HEAD_DIM], F32)
                for i in range(2):
                    if s // COUPLES != 1:
                        b, a = divmod(s, COUPLES)
                        product(bank[:, i, :], b, a * COUPLE + part, i, 0, HEAD_DIM)
                    else:
                        b, h, q = divide(s)
                        product(bank[:, i, :], b, (2 * q + part) * COUPLE + i, h, 0, HEAD_DIM)
                banks.append(bank)
            state[s] = banks

        def divide(s):
            return s // COUPLES, s % COUPLES // 2, s % 2

        def multiply_rows(s, j, t0, t1):
            b, a = divmod(s, COUPLES)
            h, i = divmod(j, HEAD_ROW_TILES)
            bank = block_banks.tile([P, BLOCK_HEADS, HEAD_DIM], F32)
            for t in range(t0, t1):
                product(bank[:, 0, t * P : (t + 1) * P], b, a * COUPLE + t, h, i * P, (i + 1) * P)
            state[s, "rows", j, t0] = bank

        def rotate_rows(s, j, t0, t1):
            b, a = divmod(s, COUPLES)
            h, i = divmod(j, HEAD_ROW_TILES)
            tiles = slice(a * COUPLE + t0, a * COUPLE + t1)
            columns = slice(i * P, (i + 1) * P)
            with_cos, with_sin, rotated = state["products", s]
            bank = state[s, "rows", j, t0][:, 0, :].rearrange("p (t d) -> p t d", t=COUPLE)
            rotate(
                blocks[b][0], bank[:, t0:t1, :],
                pairs(cos_sb[:, tiles, columns]), pairs(sin_sb[:, tiles, columns]),
                with_cos[:, h, t0:t1, columns], with_sin[:, h, t0:t1, columns],
            )

        def new_products(s):
            with_cos = products.tile([P, BLOCK_HEADS, COUPLE, HEAD_DIM], F32)
            with_sin = products.tile([P, BLOCK_HEADS, COUPLE, HEAD_DIM], F32)
            rotated = results.tile([P, BLOCK_HEADS, COUPLE, HEAD_DIM], F32)
            state["products", s] = (with_cos, with_sin, rotated)

        def rotate_part_shared(s, part):
            b, a = divmod(s, COUPLES)
            n = a * COUPLE + part
            with_cos, with_sin, rotated = state["products", s]
            bank = state[s][part]
            copied = copies.tile([P, BLOCK_HEADS, HEAD_DIM], F32)
            nc.scalar.mul(out=copied[:], in_=bank[:], mul=scalings[blocks[b][0]])
            nc.gpsimd.tensor_tensor(
                out=pairs(with_sin[:, :, part, :]), in0=pairs(copied[:])[:, :, :, ::-1],
                in1=table_for_heads(sin_sb, n), op=MULT,
            )
            nc.vector.scalar_tensor_tensor(
                out=pairs(with_cos[:, :, part, :]), in0=pairs(bank[:]), scalar=scalings[blocks[b][0]],
                in1=table_for_heads(cos_sb, n), op0=MULT, op1=MULT,
            )

        def rotate_part(s, part):
            with_cos, with_sin, rotated = state["products", s]
            if s // COUPLES != 1:
                b, a = divmod(s, COUPLES)
                n = a * COUPLE + part
                rotate(
                    blocks[b][0], state[s][part][:], table_for_heads(cos_sb, n),
                    table_for_heads(sin_sb, n), with_cos[:, :, part, :], with_sin[:, :, part, :],
                )
            else:
                b, h, q = divide(s)
                first = (2 * q + part) * COUPLE
                tiles = slice(first, first + COUPLE)
                rotate(
                    blocks[b][0], state[s][part][:], pairs(cos_sb[:, tiles, :]),
                    pairs(sin_sb[:, tiles, :]), with_cos[:, part, :, :], with_sin[:, part, :, :],
                )

        def add(s, engine, h0, h1):
            with_cos, with_sin, rotated = state["products", s]
            engine.tensor_tensor(
                out=rotated[:, h0:h1, :, :], in0=with_cos[:, h0:h1, :, :],
                in1=with_sin[:, h0:h1, :, :], op=ADD,
            )

        def add_by_tensor(s, h):
            with_cos, with_sin, rotated = state["products", s]
            turned = turn_banks.tile([P, PASSES, HALVES, P], F32)
            bank = turned[:].rearrange("p g u r -> p (g u r)")
            for i, product_tile in enumerate((with_cos, with_sin)):
                nc.tensor.matmul(
                    out=bank, lhsT=identity[:],
                    rhs=product_tile[:, h, :, :].rearrange("p t d -> p (t d)"),
                    start=(i == 0), stop=(i == 1),
                )
            nc.scalar.copy(out=rotated[:, h, :, :].rearrange("p t d -> p (t d)"), in_=bank)

        def store(s, h0, h1):
            if s // COUPLES != 1:
                b, a = divmod(s, COUPLES)
                m, c = blocks[b]
                rows = couple_rows[m][c, a][:, h0:h1, :]
            else:
                b, h, q = divide(s)
                m, c = blocks[b]
                rows = head_rows[m][c * BLOCK_HEADS + h][:, 2 * q + h0 : 2 * q + h1, :]
            rotated = state["products", s][2]
            nc.sync.dma_start(
                out=rows, in_=rotated[:, h0:h1, :, :].rearrange("p h t d -> p h (t d)")
            )

        by_scalar = nc.scalar.copy
        by_vector = nc.vector.tensor_copy

        load_tokens(0, 0, 1)
        load_rows(0, 0, 0, 1)
        load_tokens(0, 1, 2)
        load_rows(0, 0, 1, 2)
        load_rows(0, 1, 0, 1)
        load_tables(0, 2)
        load_rows(0, 1, 1, 2)
        load_tokens(1, 0, 1)
        load_tokens(1, 1, 2)
        load_tokens(2, 0, 2)
        load_tables(2, 4)
        load_tokens(3, 0, 2)
        load_tables(4, 8)
        for b in range(1, len(blocks)):
            for h in range(BLOCK_HEADS):
                load_rows(b, h, 0, HEAD_ROW_TILES)

        new_products(0)
        turn_token(0, by_vector)
        turn_first_rows(0, by_vector)
        quantise_first_rows(0)
        quantise_tokens(0, 0, 1)
        turn_token(1, by_scalar)
        turn_first_rows(1, by_scalar)
        negate_even_sines(0, 2)
        turn_first_rows(2, by_scalar)
        multiply_rows(0, 0, 0, 1)
        quantise_tokens(0, 1, 2)
        multiply_rows(0, 0, 1, 2)
        quantise_first_rows(1)
        rotate_rows(0, 0, 0, 1)
        rotate_rows(0, 0, 1, 2)
        turn_first_rows(3, by_scalar)
        multiply_rows(0, 1, 0, 2)
        quantise_first_rows(2)
        turn_token(2, by_scalar)
        turn_token(3, by_scalar)
        multiply_rows(0, 2, 0, 2)
        rotate_rows(0, 1, 0, 2)
        quantise_first_rows(3)
        turn_token(4, by_scalar)
        turn_token(5, by_scalar)
        multiply_rows(0, 3, 0, 2)
        negate_even_sines(2, 4)
        rotate_rows(0, 2, 0, 2)
        quantise_tokens(1, 0, 2)
        turn_token(6, by_scalar)
        multiply(1)
        turn_token(7, by_scalar)
        negate_even_sines(4, 8)
        rotate_rows(0, 3, 0, 2)
        quantise_tokens(2, 0, 2)
        add(0, nc.gpsimd, 0, 2)
        store(0, 0, 2)

        last = len(blocks) * COUPLES - 1
        by_tensor = {(COUPLES + 1, 1), (2 * COUPLES + 1, 1), (3 * COUPLES, 1), (last - 1, 1)}
        for s in range(1, last):
            new_products(s)
            multiply(s + 1)
            b, a = divmod(s, COUPLES)
            if b == 0 and a > 0 and a < 3:
                for i in range(HEAD_ROW_TILES):
                    turn_rows(1, a - 1, i, by_scalar)
            if b > 0 and b + 1 < len(blocks) and a < 2:
                for i in range(HEAD_ROW_TILES):
                    turn_rows(b + 1, a, i, by_scalar)
            for h in range(2):
                if (s - 1, h) in by_tensor:
                    add_by_tensor(s - 1, h)
                    store(s - 1, h, h + 1)
            for part in range(2):
                (rotate_part_shared if (s, part) in ((3 * COUPLES - 1, 1),) else rotate_part)(s, part)
            if s == 1:
                quantise_tokens(3, 0, 2)
            if s == 2:
                quantise_heads(1, 0, 1)
            if s == 3:
                quantise_heads(1, 1, 2)
            if b > 0 and b + 1 < len(blocks) and a == 2:
                quantise_heads(b + 1, 0, 2)
            heads = [h for h in range(2) if (s, h) not in by_tensor]
            add(s, nc.gpsimd, heads[0], heads[-1] + 1)
            store(s, heads[0], heads[-1] + 1)

        new_products(last)
        for h in range(2):
            if (last - 1, h) in by_tensor:
                add_by_tensor(last - 1, h)
                store(last - 1, h, h + 1)
        rotate_part(last, 0)
        rotate_part(last, 1)
        add(last, nc.vector, 0, 1)
        store(last, 0, 1)
        add(last, nc.vector, 1, 2)
        store(last, 1, 2)
